import numpy as np
import ml_dtypes


def mxq(x, axis, fmt="e4m3"):
    dtype, down = {"e4m3": (ml_dtypes.float8_e4m3fn, 7), "e5m2": (ml_dtypes.float8_e5m2, 14)}[fmt]
    v = np.moveaxis(np.asarray(x, np.float32).astype(ml_dtypes.bfloat16).astype(np.float64), axis, -1)
    blocks = v.reshape(v.shape[:-1] + (-1, 32))
    amax = np.abs(blocks).max(-1, keepdims=True)
    byte = np.maximum(np.where(amax > 0, np.frexp(amax)[1] - 1 + 127, 0) - down, 1)
    scale = np.exp2(byte - 127.0)
    codes = (blocks / scale).astype(np.float32).astype(dtype).astype(np.float64)
    return np.moveaxis((codes * scale).reshape(v.shape), -1, axis)


WIDE = False


def mx_kscale(k):
    if not WIDE:
        return np.ones(k)
    levels = np.array([10, -10, 5, -5, 0])
    a = np.random.permutation(np.resize(levels, k // 512 * 4)).reshape(k // 512, 4)
    idx = np.arange(k)
    return np.exp2(a[idx // 512, idx % 128 // 32])


BF16 = ml_dtypes.bfloat16


def bf(x):
    return np.asarray(x, np.float32).astype(BF16)


def f64(x):
    return np.asarray(x).astype(np.float64)


B, IDIM, HDIM, ODIM, S, DEPTH, NACT, NTOP = 1024, 512, 1024, 512, 128, 32, 3, 2


def sigmoid(v):
    return 1.0 / (1.0 + np.exp(-v))


def setup_inputs():
    s, t = mx_kscale(IDIM), mx_kscale(HDIM)
    return {"x": bf(np.random.standard_normal((B, IDIM)) * s),
            "hidden": bf(np.random.standard_normal((B, HDIM)) * t),
            "stack_top": bf(np.random.standard_normal((B, NTOP, S))),
            "Wi": bf(np.random.standard_normal((HDIM, IDIM)) * 0.7 / np.sqrt(IDIM) / s),
            "bi": bf(np.random.standard_normal(HDIM) * 0.2),
            "Wh": bf(np.random.standard_normal((HDIM, HDIM)) * 0.7 / np.sqrt(HDIM) / t),
            "bh": bf(np.random.standard_normal(HDIM) * 0.2),
            "W0": bf(np.random.standard_normal((HDIM, S)) * 0.5 / np.sqrt(S)),
            "b0": bf(np.random.standard_normal(HDIM) * 0.2),
            "W1": bf(np.random.standard_normal((HDIM, S)) * 0.5 / np.sqrt(S)),
            "b1": bf(np.random.standard_normal(HDIM) * 0.2)}


def reference(x, hidden, stack_top, Wi, bi, Wh, bh, W0, b0, W1, b1):
    pre = ((mxq(f64(x), 1, "e4m3") @ mxq(f64(Wi), 1, "e4m3").T) + f64(bi)
           + (mxq(f64(hidden), 1, "e4m3") @ mxq(f64(Wh), 1, "e4m3").T) + f64(bh)
           + f64(stack_top)[:, 0] @ f64(W0).T + f64(b0)
           + f64(stack_top)[:, 1] @ f64(W1).T + f64(b1))
    return sigmoid(pre)

@@ -1,0 +1,214 @@
+from contextlib import ExitStack
+
+import concourse.mybir as mybir
+from concourse.masks import make_identity
+
+F32 = mybir.dt.float32
+BF16 = mybir.dt.bfloat16
+U32 = mybir.dt.uint32
+U8 = mybir.dt.uint8
+FP8X4 = mybir.dt.float8_e4m3fn_x4
+ADD = mybir.AluOpType.add
+SIGMOID = mybir.ActivationFunctionType.Sigmoid
+
+P = 128
+B, IDIM, HDIM, S = 1024, 512, 1024, 128
+NB = B // P
+PASSES = 3
+FLOPS = 2 * B * HDIM * (IDIM + HDIM + 2 * S)
+
+
+def tile_stackrnn_pa_kernel(tc, x, hidden, stack_top, Wi, bi, Wh, bh, W0, b0, W1, b1, out):
+    nc = tc.nc
+    with ExitStack() as ctx:
+        keep = ctx.enter_context(tc.tile_pool(name="keep", bufs=1))
+        tp_pool = ctx.enter_context(tc.psum_pool(name="tp", bufs=3))
+        pl_pool = ctx.enter_context(tc.psum_pool(name="pl", bufs=2))
+        mx_pool = ctx.enter_context(tc.psum_pool(name="mx", bufs=3))
+
+        x_sb = keep.tile([P, NB * IDIM], BF16)
+        h_sb = keep.tile([P, NB * HDIM], BF16)
+        st_sb = keep.tile([P, NB * 2 * S], BF16)
+        wi_sb = keep.tile([P, 8 * IDIM], BF16)
+        wh_sb = keep.tile([P, 8 * HDIM], BF16)
+        w01_sb = keep.tile([P, 2, 2, 4, S], BF16)
+        bias_rows = keep.tile([P, HDIM], BF16)
+        ones = keep.tile([P, P], BF16)
+        ident_b = keep.tile([P, P], BF16)
+        ident_f = keep.tile([P, P], F32)
+        warm = keep.tile([P, 1], F32)
+        stT = keep.tile([P, NB * 2 * P], BF16)
+        w01T = keep.tile([P, 2, 2, 512], BF16)
+        bias_bc = keep.tile([P, HDIM], F32)
+        a_codes = keep.tile([P, PASSES, B], U32, align_bytes=64)
+        a_scales = keep.tile([P, PASSES, B], U8, align_bytes=64)
+        w_codes = keep.tile([P, PASSES, HDIM], U32, align_bytes=64)
+        w_scales = keep.tile([P, PASSES, HDIM], U8, align_bytes=64)
+        pre = keep.tile([P, NB, HDIM], F32)
+
+        nc.vector.memset(bias_rows[:], 0.0)
+        nc.vector.memset(ones[:], 1.0)
+        nc.vector.memset(warm[:], 0.0)
+        make_identity(nc, ident_b[:])
+        make_identity(nc, ident_f[:])
+        for r, b_vec in enumerate((bi, bh, b0, b1)):
+            nc.scalar.dma_start(out=bias_rows[r : r + 1, :], in_=b_vec.rearrange("(o n) -> o n", o=1))
+        nc.scalar.activation(out=warm[:], in_=warm[:], func=SIGMOID)
+
+        st_v = stack_top.rearrange("(p t) s k -> p (t s k)", t=NB)
+        w0_v = W0.rearrange("(n t p) k -> p n t k", n=2, t=4)
+        w1_v = W1.rearrange("(n t p) k -> p n t k", n=2, t=4)
+        x_v = x.rearrange("(p t) k -> p (t k)", t=NB)
+        h_v = hidden.rearrange("(p t) k -> p (t k)", t=NB)
+        wi_v = Wi.rearrange("(g p t) k -> p g (t k)", g=4, t=2)
+        wh_v = Wh.rearrange("(g p t) k -> p g (t k)", g=4, t=2)
+        wi_t = wi_sb[:].rearrange("p (g c) -> p g c", g=4)
+
+        for half in range(2):
+            nc.sync.dma_start(out=st_sb[:, half * 1024 : (half + 1) * 1024], in_=st_v[:, half * 1024 : (half + 1) * 1024])
+            nc.sync.dma_start(out=w01_sb[:, half, 0], in_=w0_v[:, half])
+            nc.sync.dma_start(out=w01_sb[:, half, 1], in_=w1_v[:, half])
+        for gg in range(2):
+            nc.sync.dma_start(out=wi_t[:, 2 * gg : 2 * gg + 2, :], in_=wi_v[:, 2 * gg : 2 * gg + 2, :])
+            for g in (2 * gg, 2 * gg + 1):
+                nc.sync.dma_start(out=wh_sb[:, g * 2048 : (g + 1) * 2048], in_=wh_v[:, g, :])
+        for hh in range(2):
+            nc.sync.dma_start(out=x_sb[:, hh * 2048 : (hh + 1) * 2048], in_=x_v[:, hh * 2048 : (hh + 1) * 2048])
+            for pr in (2 * hh, 2 * hh + 1):
+                nc.sync.dma_start(out=h_sb[:, pr * 2048 : (pr + 1) * 2048], in_=h_v[:, pr * 2048 : (pr + 1) * 2048])
+
+        def stack_bank(blocks, dst, engine):
+            bank = tp_pool.tile([P, 8 * P], BF16, tag="tp", name="sbank")
+            for i, blk in enumerate(blocks):
+                nc.tensor.transpose(bank[:, i * P : (i + 1) * P], blk, ident_b[:])
+            if engine == "v":
+                nc.vector.tensor_copy(out=dst, in_=bank[:])
+            else:
+                nc.scalar.copy(out=dst, in_=bank[:])
+
+        def st_bank(half):
+            stack_bank(
+                [st_sb[:, (8 * half + i) * P : (8 * half + i + 1) * P] for i in range(8)],
+                stT[:, half * 1024 : (half + 1) * 1024],
+                "v",
+            )
+
+        def w01_bank(n):
+            stack_bank(
+                [w01_sb[:, n, s, tl, :] for s in range(2) for tl in range(4)],
+                w01T[:, n].rearrange("p s h -> p (s h)"),
+                "s",
+            )
+
+        def bias_spread():
+            for n in range(2):
+                bank = pl_pool.tile([P, 512], F32, tag="pl", name="bbank")
+                nc.tensor.matmul(bank[:], lhsT=ones[:], rhs=bias_rows[:, n * 512 : (n + 1) * 512], start=True, stop=True)
+                nc.vector.tensor_copy(out=bias_bc[:, n * 512 : (n + 1) * 512], in_=bank[:])
+
+        def plain(m, n):
+            bank = pl_pool.tile([P, 512], F32, tag="pl", name="pbank")
+            for s in range(2):
+                nc.tensor.matmul(
+                    bank[:],
+                    lhsT=stT[:, (2 * m + s) * P : (2 * m + s + 1) * P],
+                    rhs=w01T[:, n, s, :],
+                    start=(s == 0),
+                    stop=(s == 1),
+                )
+            cols = slice(n * 512, (n + 1) * 512)
+            nc.vector.tensor_tensor(out=pre[:, m, cols], in0=bank[:], in1=bias_bc[:, cols], op=ADD)
+
+        xw = x_sb[:].bitcast(F32)
+        hw = h_sb[:].bitcast(F32)
+        wiw = wi_sb[:].bitcast(F32)
+        whw = wh_sb[:].bitcast(F32)
+
+        def mx_bank(kind, c, q):
+            if c == 0:
+                src, row_words, off = (xw if kind == "a" else wiw), IDIM // 2, 0
+            else:
+                src, row_words, off = (hw if kind == "a" else whw), HDIM // 2, (c - 1) * 256
+            bank = tp_pool.tile([P, 512], F32, tag="tp", name="tbank")
+            for r in range(2):
+                for u in range(2):
+                    start = (2 * q + r) * row_words + off + u * P
+                    nc.tensor.transpose(bank[:, (2 * r + u) * P : (2 * r + u + 1) * P], src[:, start : start + P], ident_f[:])
+            grouped = keep.tile([P, 1024], BF16, align_bytes=64, name="grp_%s%d%d" % (kind, c, q))
+            gw = grouped[:].bitcast(F32)
+            if kind == "a":
+                nc.scalar.copy(
+                    out=gw.rearrange("p (r j u) -> p r j u", r=2, u=2),
+                    in_=bank[:].rearrange("p (r u j) -> p r j u", r=2, u=2),
+                )
+                codes, scales = a_codes, a_scales
+            else:
+                nc.scalar.copy(
+                    out=gw.rearrange("p (j r u) -> p j r u", r=2, u=2),
+                    in_=bank[:].rearrange("p (r u j) -> p j r u", r=2, u=2),
+                )
+                codes, scales = w_codes, w_scales
+            cols = slice(q * 256, (q + 1) * 256)
+            return (codes[:, c, cols], scales[:, c, cols], grouped)
+
+        def quantise(job):
+            codes, scales, grouped = job
+            nc.vector.quantize_mx(out=codes.bitcast(FP8X4), scales=scales, in_=grouped[:])
+
+        out_v = out.rearrange("(p t) h -> p t h", t=NB)
+
+        def mx_group(m, n):
+            bank = mx_pool.tile([P, 512], F32, tag="mx", name="mbank")
+            rows = slice(m * P, (m + 1) * P)
+            cols = slice(n * 512, (n + 1) * 512)
+            for c in range(PASSES):
+                nc.tensor.matmul_mx(
+                    out=bank[:],
+                    lhsT=a_codes[:, c, rows].bitcast(FP8X4),
+                    lhsT_scale=a_scales[:, c, rows],
+                    rhs=w_codes[:, c, cols].bitcast(FP8X4),
+                    rhs_scale=w_scales[:, c, cols],
+                    start=(c == 0),
+                    stop=(c == PASSES - 1),
+                )
+            nc.vector.tensor_tensor(out=pre[:, m, cols], in0=bank[:], in1=pre[:, m, cols], op=ADD)
+
+        st_bank(0)
+        w01_bank(0)
+        bias_spread()
+        st_bank(1)
+        w01_bank(1)
+
+        plain_list = [(m, 0) for m in range(4)] + [(m, 1) for m in range(4)] + [(m, n) for m in range(4, 8) for n in range(2)]
+        chunks = []
+        for gg in range(2):
+            chunks.append([("w", 0, 2 * gg), ("w", 0, 2 * gg + 1)])
+            for g in (2 * gg, 2 * gg + 1):
+                chunks.append([("w", 1, g), ("w", 2, g)])
+        for hh in range(2):
+            chunks.append([("a", 0, 2 * hh), ("a", 0, 2 * hh + 1)])
+            for pr in (2 * hh, 2 * hh + 1):
+                chunks.append([("a", 1, pr), ("a", 2, pr)])
+
+        for i in range(4):
+            plain(*plain_list[i])
+        jobs = []
+        for i, chunk in enumerate(chunks):
+            for kind, c, q in chunk:
+                jobs.append(mx_bank(kind, c, q))
+                if len(jobs) > 1:
+                    quantise(jobs[-2])
+            plain(*plain_list[4 + i])
+        quantise(jobs[-1])
+
+        for m in range(NB):
+            for n in range(2):
+                mx_group(m, n)
+            if m < NB - 1:
+                nc.scalar.activation(out=pre[:, m, :], in_=pre[:, m, :], func=SIGMOID)
+                nc.sync.dma_start(out=out_v[:, m, :], in_=pre[:, m, :])
+            else:
+                for n in range(2):
+                    cols = slice(n * 512, (n + 1) * 512)
+                    nc.scalar.activation(out=pre[:, m, cols], in_=pre[:, m, cols], func=SIGMOID)
+                    nc.sync.dma_start(out=out_v[:, m, cols], in_=pre[:, m, cols])

@@ -25,20 +25,20 @@ def tile_stackrnn_pa_kernel(tc, x, hidden, stack_top, Wi, bi, Wh, bh, W0, b0, W1
         tp_pool = ctx.enter_context(tc.psum_pool(name="tp", bufs=3))
         pl_pool = ctx.enter_context(tc.psum_pool(name="pl", bufs=2))
         mx_pool = ctx.enter_context(tc.psum_pool(name="mx", bufs=3))
+        ctx.enter_context(tc.manual_schedule())
 
         x_sb = keep.tile([P, NB * IDIM], BF16)
         h_sb = keep.tile([P, NB * HDIM], BF16)
         st_sb = keep.tile([P, NB * 2 * S], BF16)
         wi_sb = keep.tile([P, 8 * IDIM], BF16)
         wh_sb = keep.tile([P, 8 * HDIM], BF16)
-        w01_sb = keep.tile([P, 2, 2, 4, S], BF16)
+        w01_sb = keep.tile([P, 2 * 4 * 2 * S], BF16)
         bias_rows = keep.tile([P, HDIM], BF16)
         ones = keep.tile([P, P], BF16)
-        ident_b = keep.tile([P, P], BF16)
         ident_f = keep.tile([P, P], F32)
         warm = keep.tile([P, 1], F32)
-        stT = keep.tile([P, NB * 2 * P], BF16)
-        w01T = keep.tile([P, 2, 2, 512], BF16)
+        stT = keep.tile([P, NB * P * 2], BF16)
+        w01T = keep.tile([P, HDIM * 2], BF16)
         bias_bc = keep.tile([P, HDIM], F32)
         a_codes = keep.tile([P, PASSES, B], U32, align_bytes=64)
         a_scales = keep.tile([P, PASSES, B], U8, align_bytes=64)
@@ -49,7 +49,6 @@ def tile_stackrnn_pa_kernel(tc, x, hidden, stack_top, Wi, bi, Wh, bh, W0, b0, W1
         nc.vector.memset(bias_rows[:], 0.0)
         nc.vector.memset(ones[:], 1.0)
         nc.vector.memset(warm[:], 0.0)
-        make_identity(nc, ident_b[:])
         make_identity(nc, ident_f[:])
         for r, b_vec in enumerate((bi, bh, b0, b1)):
             nc.scalar.dma_start(out=bias_rows[r : r + 1, :], in_=b_vec.rearrange("(o n) -> o n", o=1))
@@ -58,6 +57,7 @@ def tile_stackrnn_pa_kernel(tc, x, hidden, stack_top, Wi, bi, Wh, bh, W0, b0, W1
         st_v = stack_top.rearrange("(p t) s k -> p (t s k)", t=NB)
         w0_v = W0.rearrange("(n t p) k -> p n t k", n=2, t=4)
         w1_v = W1.rearrange("(n t p) k -> p n t k", n=2, t=4)
+        w01_t = w01_sb[:].rearrange("p (n t s k) -> p n t s k", n=2, t=4, s=2)
         x_v = x.rearrange("(p t) k -> p (t k)", t=NB)
         h_v = hidden.rearrange("(p t) k -> p (t k)", t=NB)
         wi_v = Wi.rearrange("(g p t) k -> p g (t k)", g=4, t=2)
@@ -66,8 +66,8 @@ def tile_stackrnn_pa_kernel(tc, x, hidden, stack_top, Wi, bi, Wh, bh, W0, b0, W1
 
         for half in range(2):
             nc.sync.dma_start(out=st_sb[:, half * 1024 : (half + 1) * 1024], in_=st_v[:, half * 1024 : (half + 1) * 1024])
-            nc.sync.dma_start(out=w01_sb[:, half, 0], in_=w0_v[:, half])
-            nc.sync.dma_start(out=w01_sb[:, half, 1], in_=w1_v[:, half])
+            nc.sync.dma_start(out=w01_t[:, half, :, 0, :], in_=w0_v[:, half])
+            nc.sync.dma_start(out=w01_t[:, half, :, 1, :], in_=w1_v[:, half])
         for gg in range(2):
             nc.sync.dma_start(out=wi_t[:, 2 * gg : 2 * gg + 2, :], in_=wi_v[:, 2 * gg : 2 * gg + 2, :])
             for g in (2 * gg, 2 * gg + 1):
@@ -77,85 +77,84 @@ def tile_stackrnn_pa_kernel(tc, x, hidden, stack_top, Wi, bi, Wh, bh, W0, b0, W1
             for pr in (2 * hh, 2 * hh + 1):
                 nc.sync.dma_start(out=h_sb[:, pr * 2048 : (pr + 1) * 2048], in_=h_v[:, pr * 2048 : (pr + 1) * 2048])
 
-        def stack_bank(blocks, dst, engine):
-            bank = tp_pool.tile([P, 8 * P], BF16, tag="tp", name="sbank")
-            for i, blk in enumerate(blocks):
-                nc.tensor.transpose(bank[:, i * P : (i + 1) * P], blk, ident_b[:])
-            if engine == "v":
-                nc.vector.tensor_copy(out=dst, in_=bank[:])
+        words = {"s": st_sb[:].bitcast(F32), "v": w01_sb[:].bitcast(F32)}
+        mx_words = {("a", 0): x_sb[:].bitcast(F32), ("a", 1): h_sb[:].bitcast(F32), ("w", 0): wi_sb[:].bitcast(F32), ("w", 1): wh_sb[:].bitcast(F32)}
+        stT_w = stT[:].bitcast(F32)
+        w01T_w = w01T[:].bitcast(F32)
+        stT_e = stT[:].rearrange("p (t j e) -> p t j e", t=NB, e=2)
+        w01T_e = w01T[:].rearrange("p (n h e) -> p n h e", n=2, e=2)
+        out_v = out.rearrange("(p t) h -> p t h", t=NB)
+        grouped = {}
+        banks = {}
+
+        def sources(kind, c, q):
+            if kind in ("s", "v"):
+                return [words[kind][:, (4 * q + i) * P : (4 * q + i + 1) * P] for i in range(4)]
+            src = mx_words[(kind, min(c, 1))]
+            row_words = IDIM // 2 if c == 0 else HDIM // 2
+            off = 0 if c == 0 else (c - 1) * 256
+            return [
+                src[:, (2 * q + r) * row_words + off + u * P : (2 * q + r) * row_words + off + (u + 1) * P]
+                for r in range(2)
+                for u in range(2)
+            ]
+
+        def transposes(job, first, last):
+            if first == 0:
+                banks[job] = tp_pool.tile([P, 512], F32, tag="tp", name="tbank")
+            srcs = sources(*job)
+            for i in range(first, last):
+                nc.tensor.transpose(banks[job][:, i * P : (i + 1) * P], srcs[i], ident_f[:])
+
+        def copy_out(job, on_vector=False):
+            kind, c, q = job
+            bank = banks[job]
+            if kind == "s":
+                dst, src = stT_w[:, q * 512 : (q + 1) * 512], bank[:]
+            elif kind == "v":
+                dst, src = w01T_w[:, q * 512 : (q + 1) * 512], bank[:]
             else:
-                nc.scalar.copy(out=dst, in_=bank[:])
-
-        def st_bank(half):
-            stack_bank(
-                [st_sb[:, (8 * half + i) * P : (8 * half + i + 1) * P] for i in range(8)],
-                stT[:, half * 1024 : (half + 1) * 1024],
-                "v",
-            )
-
-        def w01_bank(n):
-            stack_bank(
-                [w01_sb[:, n, s, tl, :] for s in range(2) for tl in range(4)],
-                w01T[:, n].rearrange("p s h -> p (s h)"),
-                "s",
-            )
-
-        def bias_spread():
-            for n in range(2):
-                bank = pl_pool.tile([P, 512], F32, tag="pl", name="bbank")
-                nc.tensor.matmul(bank[:], lhsT=ones[:], rhs=bias_rows[:, n * 512 : (n + 1) * 512], start=True, stop=True)
-                nc.vector.tensor_copy(out=bias_bc[:, n * 512 : (n + 1) * 512], in_=bank[:])
-
-        def plain(m, n):
-            bank = pl_pool.tile([P, 512], F32, tag="pl", name="pbank")
-            for s in range(2):
-                nc.tensor.matmul(
-                    bank[:],
-                    lhsT=stT[:, (2 * m + s) * P : (2 * m + s + 1) * P],
-                    rhs=w01T[:, n, s, :],
-                    start=(s == 0),
-                    stop=(s == 1),
-                )
-            cols = slice(n * 512, (n + 1) * 512)
-            nc.vector.tensor_tensor(out=pre[:, m, cols], in0=bank[:], in1=bias_bc[:, cols], op=ADD)
-
-        xw = x_sb[:].bitcast(F32)
-        hw = h_sb[:].bitcast(F32)
-        wiw = wi_sb[:].bitcast(F32)
-        whw = wh_sb[:].bitcast(F32)
-
-        def mx_bank(kind, c, q):
-            if c == 0:
-                src, row_words, off = (xw if kind == "a" else wiw), IDIM // 2, 0
+                grouped[job] = keep.tile([P, 1024], BF16, align_bytes=64, name="grp_%s%d%d" % job)
+                gw = grouped[job][:].bitcast(F32)
+                if kind == "a":
+                    dst = gw.rearrange("p (r j u) -> p r j u", r=2, u=2)
+                    src = bank[:].rearrange("p (r u j) -> p r j u", r=2, u=2)
+                else:
+                    dst = gw.rearrange("p (j r u) -> p j r u", r=2, u=2)
+                    src = bank[:].rearrange("p (r u j) -> p j r u", r=2, u=2)
+            if on_vector:
+                nc.vector.tensor_copy(out=dst, in_=src)
             else:
-                src, row_words, off = (hw if kind == "a" else whw), HDIM // 2, (c - 1) * 256
-            bank = tp_pool.tile([P, 512], F32, tag="tp", name="tbank")
-            for r in range(2):
-                for u in range(2):
-                    start = (2 * q + r) * row_words + off + u * P
-                    nc.tensor.transpose(bank[:, (2 * r + u) * P : (2 * r + u + 1) * P], src[:, start : start + P], ident_f[:])
-            grouped = keep.tile([P, 1024], BF16, align_bytes=64, name="grp_%s%d%d" % (kind, c, q))
-            gw = grouped[:].bitcast(F32)
-            if kind == "a":
-                nc.scalar.copy(
-                    out=gw.rearrange("p (r j u) -> p r j u", r=2, u=2),
-                    in_=bank[:].rearrange("p (r u j) -> p r j u", r=2, u=2),
-                )
-                codes, scales = a_codes, a_scales
-            else:
-                nc.scalar.copy(
-                    out=gw.rearrange("p (j r u) -> p j r u", r=2, u=2),
-                    in_=bank[:].rearrange("p (r u j) -> p j r u", r=2, u=2),
-                )
-                codes, scales = w_codes, w_scales
-            cols = slice(q * 256, (q + 1) * 256)
-            return (codes[:, c, cols], scales[:, c, cols], grouped)
+                nc.scalar.copy(out=dst, in_=src)
 
         def quantise(job):
-            codes, scales, grouped = job
-            nc.vector.quantize_mx(out=codes.bitcast(FP8X4), scales=scales, in_=grouped[:])
+            kind, c, q = job
+            codes, scales = (a_codes, a_scales) if kind == "a" else (w_codes, w_scales)
+            cols = slice(q * 256, (q + 1) * 256)
+            nc.vector.quantize_mx(out=codes[:, c, cols].bitcast(FP8X4), scales=scales[:, c, cols], in_=grouped[job][:])
 
-        out_v = out.rearrange("(p t) h -> p t h", t=NB)
+        def plain_matmul(group, e):
+            m, n = group
+            if e == 0:
+                banks[group] = pl_pool.tile([P, 512], F32, tag="pl", name="pbank")
+            nc.tensor.matmul(banks[group][:], lhsT=stT_e[:, m, :, e], rhs=w01T_e[:, n, :, e], start=(e == 0), stop=(e == 1))
+
+        def add_bias(group):
+            m, n = group
+            cols = slice(n * 512, (n + 1) * 512)
+            nc.vector.tensor_tensor(out=pre[:, m, cols], in0=banks[group][:], in1=bias_bc[:, cols], op=ADD)
+
+        def bank_alone(job, on_vector=False):
+            transposes(job, 0, 4)
+            copy_out(job, on_vector)
+
+        def woven(group, job):
+            plain_matmul(group, 0)
+            transposes(job, 0, 2)
+            plain_matmul(group, 1)
+            transposes(job, 2, 4)
+            copy_out(job)
+            add_bias(group)
 
         def mx_group(m, n):
             bank = mx_pool.tile([P, 512], F32, tag="mx", name="mbank")
@@ -173,42 +172,64 @@ def tile_stackrnn_pa_kernel(tc, x, hidden, stack_top, Wi, bi, Wh, bh, W0, b0, W1
                 )
             nc.vector.tensor_tensor(out=pre[:, m, cols], in0=bank[:], in1=pre[:, m, cols], op=ADD)
 
-        st_bank(0)
-        w01_bank(0)
-        bias_spread()
-        st_bank(1)
-        w01_bank(1)
+        def finish(m, first_col, last_col):
+            cols = slice(first_col, last_col)
+            nc.scalar.activation(out=pre[:, m, cols], in_=pre[:, m, cols], func=SIGMOID)
+            nc.sync.dma_start(out=out_v[:, m, cols], in_=pre[:, m, cols])
 
-        plain_list = [(m, 0) for m in range(4)] + [(m, 1) for m in range(4)] + [(m, n) for m in range(4, 8) for n in range(2)]
+        bank_alone(("s", 0, 0), on_vector=True)
+        bank_alone(("v", 0, 0))
+        bias_banks = []
+        for n in range(2):
+            bias_banks.append(mx_pool.tile([P, 512], F32, tag="mx", name="bbank"))
+            nc.tensor.matmul(bias_banks[n][:], lhsT=ones[:], rhs=bias_rows[:, n * 512 : (n + 1) * 512], start=True, stop=True)
+        nc.vector.tensor_copy(out=bias_bc[:, 0:512], in_=bias_banks[0][:])
+        nc.scalar.copy(out=bias_bc[:, 512:1024], in_=bias_banks[1][:])
+        woven((0, 0), ("s", 0, 1))
+        woven((1, 0), ("v", 0, 1))
+
+        groups = [(2, 0), (3, 0)] + [(m, 1) for m in range(4)] + [(m, n) for m in range(4, 8) for n in range(2)]
         chunks = []
-        for gg in range(2):
-            chunks.append([("w", 0, 2 * gg), ("w", 0, 2 * gg + 1)])
-            for g in (2 * gg, 2 * gg + 1):
-                chunks.append([("w", 1, g), ("w", 2, g)])
-        for hh in range(2):
-            chunks.append([("a", 0, 2 * hh), ("a", 0, 2 * hh + 1)])
-            for pr in (2 * hh, 2 * hh + 1):
-                chunks.append([("a", 1, pr), ("a", 2, pr)])
-
-        for i in range(4):
-            plain(*plain_list[i])
-        jobs = []
-        for i, chunk in enumerate(chunks):
-            for kind, c, q in chunk:
-                jobs.append(mx_bank(kind, c, q))
-                if len(jobs) > 1:
-                    quantise(jobs[-2])
-            plain(*plain_list[4 + i])
-        quantise(jobs[-1])
-
-        for m in range(NB):
-            for n in range(2):
-                mx_group(m, n)
-            if m < NB - 1:
-                nc.scalar.activation(out=pre[:, m, :], in_=pre[:, m, :], func=SIGMOID)
-                nc.sync.dma_start(out=out_v[:, m, :], in_=pre[:, m, :])
+        for kind in ("w", "a"):
+            for hh in range(2):
+                chunks.append([(kind, 0, 2 * hh), (kind, 0, 2 * hh + 1)])
+                for q in (2 * hh, 2 * hh + 1):
+                    chunks.append([(kind, 1, q), (kind, 2, q)])
+        EARLY = 10
+        gi = 0
+        for i in range(EARLY):
+            job_a, job_b = chunks[i]
+            bank_alone(job_a)
+            quantise(job_a)
+            woven(groups[gi], job_b)
+            gi += 1
+            quantise(job_b)
+            if i == 0:
+                plain_matmul(groups[gi], 0)
+                plain_matmul(groups[gi], 1)
+                add_bias(groups[gi])
+                gi += 1
+        for m in range(4):
+            mx_group(m, 0)
+            mx_group(m, 1)
+            if m < 3:
+                finish(m, 0, HDIM)
+        for i in range(EARLY, len(chunks)):
+            job_a, job_b = chunks[i]
+            if len(groups) - gi >= 2 * (len(chunks) - i):
+                woven(groups[gi], job_a)
+                gi += 1
             else:
-                for n in range(2):
-                    cols = slice(n * 512, (n + 1) * 512)
-                    nc.scalar.activation(out=pre[:, m, cols], in_=pre[:, m, cols], func=SIGMOID)
-                    nc.sync.dma_start(out=out_v[:, m, cols], in_=pre[:, m, cols])
+                bank_alone(job_a)
+            woven(groups[gi], job_b)
+            gi += 1
+            quantise(job_a)
+            quantise(job_b)
+        finish(3, 0, HDIM)
+        for m in range(4, 7):
+            mx_group(m, 0)
+            mx_group(m, 1)
+            finish(m, 0, HDIM)
+        for n in range(2):
+            mx_group(7, n)
+            finish(7, n * 512, (n + 1) * 512)

@@ -15,6 +15,7 @@ P = 128
 B, IDIM, HDIM, S = 1024, 512, 1024, 128
 NB = B // P
 PASSES = 3
+ST_SLOTS = ((0, 1), (2, 3, 4, 5), (6, 7))
 FLOPS = 2 * B * HDIM * (IDIM + HDIM + 2 * S)
 
 
@@ -64,10 +65,12 @@ def tile_stackrnn_pa_kernel(tc, x, hidden, stack_top, Wi, bi, Wh, bh, W0, b0, W1
         wh_v = Wh.rearrange("(g p t) k -> p g (t k)", g=4, t=2)
         wi_t = wi_sb[:].rearrange("p (g c) -> p g c", g=4)
 
-        for half in range(2):
-            nc.sync.dma_start(out=st_sb[:, half * 1024 : (half + 1) * 1024], in_=st_v[:, half * 1024 : (half + 1) * 1024])
-            nc.sync.dma_start(out=w01_t[:, half, :, 0, :], in_=w0_v[:, half])
-            nc.sync.dma_start(out=w01_t[:, half, :, 1, :], in_=w1_v[:, half])
+        nc.sync.dma_start(out=w01_t[:, 0, :, 0, :], in_=w0_v[:, 0])
+        nc.sync.dma_start(out=w01_t[:, 0, :, 1, :], in_=w1_v[:, 0])
+        nc.sync.dma_start(out=st_sb[:, 0:512], in_=st_v[:, 0:512])
+        nc.sync.dma_start(out=st_sb[:, 512:2048], in_=st_v[:, 512:2048])
+        nc.sync.dma_start(out=w01_t[:, 1, :, 0, :], in_=w0_v[:, 1])
+        nc.sync.dma_start(out=w01_t[:, 1, :, 1, :], in_=w1_v[:, 1])
         for gg in range(2):
             nc.sync.dma_start(out=wi_t[:, 2 * gg : 2 * gg + 2, :], in_=wi_v[:, 2 * gg : 2 * gg + 2, :])
             for g in (2 * gg, 2 * gg + 1):
@@ -88,7 +91,9 @@ def tile_stackrnn_pa_kernel(tc, x, hidden, stack_top, Wi, bi, Wh, bh, W0, b0, W1
         banks = {}
 
         def sources(kind, c, q):
-            if kind in ("s", "v"):
+            if kind == "s":
+                return [words[kind][:, t * P : (t + 1) * P] for t in ST_SLOTS[q]]
+            if kind == "v":
                 return [words[kind][:, (4 * q + i) * P : (4 * q + i + 1) * P] for i in range(4)]
             src = mx_words[(kind, min(c, 1))]
             row_words = IDIM // 2 if c == 0 else HDIM // 2
@@ -110,7 +115,8 @@ def tile_stackrnn_pa_kernel(tc, x, hidden, stack_top, Wi, bi, Wh, bh, W0, b0, W1
             kind, c, q = job
             bank = banks[job]
             if kind == "s":
-                dst, src = stT_w[:, q * 512 : (q + 1) * 512], bank[:]
+                slots = ST_SLOTS[q]
+                dst, src = stT_w[:, slots[0] * P : (slots[-1] + 1) * P], bank[:, 0 : len(slots) * P]
             elif kind == "v":
                 dst, src = w01T_w[:, q * 512 : (q + 1) * 512], bank[:]
             else:
@@ -145,18 +151,23 @@ def tile_stackrnn_pa_kernel(tc, x, hidden, stack_top, Wi, bi, Wh, bh, W0, b0, W1
             nc.vector.tensor_tensor(out=pre[:, m, cols], in0=banks[group][:], in1=bias_bc[:, cols], op=ADD)
 
         def bank_alone(job, on_vector=False):
-            transposes(job, 0, 4)
+            transposes(job, 0, len(sources(*job)))
             copy_out(job, on_vector)
 
         def woven(group, job):
             plain_matmul(group, 0)
             transposes(job, 0, 2)
             plain_matmul(group, 1)
-            transposes(job, 2, 4)
+            transposes(job, 2, len(sources(*job)))
             copy_out(job)
             add_bias(group)
 
-        def mx_group(m, n):
+        def finish(m, first_col, last_col):
+            cols = slice(first_col, last_col)
+            nc.scalar.activation(out=pre[:, m, cols], in_=pre[:, m, cols], func=SIGMOID)
+            nc.sync.dma_start(out=out_v[:, m, cols], in_=pre[:, m, cols])
+
+        def mx_group(m, n, pieces=0):
             bank = mx_pool.tile([P, 512], F32, tag="mx", name="mbank")
             rows = slice(m * P, (m + 1) * P)
             cols = slice(n * 512, (n + 1) * 512)
@@ -170,25 +181,26 @@ def tile_stackrnn_pa_kernel(tc, x, hidden, stack_top, Wi, bi, Wh, bh, W0, b0, W1
                     start=(c == 0),
                     stop=(c == PASSES - 1),
                 )
-            nc.vector.tensor_tensor(out=pre[:, m, cols], in0=bank[:], in1=pre[:, m, cols], op=ADD)
+            width = 512 // max(pieces, 1)
+            for i in range(max(pieces, 1)):
+                part = slice(n * 512 + i * width, n * 512 + (i + 1) * width)
+                nc.vector.tensor_tensor(out=pre[:, m, part], in0=bank[:, i * width : (i + 1) * width], in1=pre[:, m, part], op=ADD)
+                if pieces > 0:
+                    finish(m, n * 512 + i * width, n * 512 + (i + 1) * width)
 
-        def finish(m, first_col, last_col):
-            cols = slice(first_col, last_col)
-            nc.scalar.activation(out=pre[:, m, cols], in_=pre[:, m, cols], func=SIGMOID)
-            nc.sync.dma_start(out=out_v[:, m, cols], in_=pre[:, m, cols])
-
-        bank_alone(("s", 0, 0), on_vector=True)
-        bank_alone(("v", 0, 0))
         bias_banks = []
         for n in range(2):
             bias_banks.append(mx_pool.tile([P, 512], F32, tag="mx", name="bbank"))
             nc.tensor.matmul(bias_banks[n][:], lhsT=ones[:], rhs=bias_rows[:, n * 512 : (n + 1) * 512], start=True, stop=True)
         nc.vector.tensor_copy(out=bias_bc[:, 0:512], in_=bias_banks[0][:])
         nc.scalar.copy(out=bias_bc[:, 512:1024], in_=bias_banks[1][:])
+        bank_alone(("v", 0, 0))
+        bank_alone(("s", 0, 0), on_vector=True)
         woven((0, 0), ("s", 0, 1))
-        woven((1, 0), ("v", 0, 1))
+        woven((1, 0), ("s", 0, 2))
+        woven((2, 0), ("v", 0, 1))
 
-        groups = [(2, 0), (3, 0)] + [(m, 1) for m in range(4)] + [(m, n) for m in range(4, 8) for n in range(2)]
+        groups = [(3, 0), (4, 0), (5, 0)] + [(m, 1) for m in range(6)] + [(6, 0), (6, 1), (7, 0), (7, 1)]
         chunks = []
         for kind in ("w", "a"):
             for hh in range(2):
@@ -196,7 +208,10 @@ def tile_stackrnn_pa_kernel(tc, x, hidden, stack_top, Wi, bi, Wh, bh, W0, b0, W1
                 for q in (2 * hh, 2 * hh + 1):
                     chunks.append([(kind, 1, q), (kind, 2, q)])
         EARLY = 10
-        gi = 0
+        plain_matmul(groups[0], 0)
+        plain_matmul(groups[0], 1)
+        add_bias(groups[0])
+        gi = 1
         for i in range(EARLY):
             job_a, job_b = chunks[i]
             bank_alone(job_a)
@@ -204,11 +219,6 @@ def tile_stackrnn_pa_kernel(tc, x, hidden, stack_top, Wi, bi, Wh, bh, W0, b0, W1
             woven(groups[gi], job_b)
             gi += 1
             quantise(job_b)
-            if i == 0:
-                plain_matmul(groups[gi], 0)
-                plain_matmul(groups[gi], 1)
-                add_bias(groups[gi])
-                gi += 1
         for m in range(4):
             mx_group(m, 0)
             mx_group(m, 1)
@@ -216,20 +226,15 @@ def tile_stackrnn_pa_kernel(tc, x, hidden, stack_top, Wi, bi, Wh, bh, W0, b0, W1
                 finish(m, 0, HDIM)
         for i in range(EARLY, len(chunks)):
             job_a, job_b = chunks[i]
-            if len(groups) - gi >= 2 * (len(chunks) - i):
-                woven(groups[gi], job_a)
-                gi += 1
-            else:
-                bank_alone(job_a)
+            bank_alone(job_a)
             woven(groups[gi], job_b)
             gi += 1
             quantise(job_a)
             quantise(job_b)
         finish(3, 0, HDIM)
-        for m in range(4, 7):
-            mx_group(m, 0)
-            mx_group(m, 1)
-            finish(m, 0, HDIM)
-        for n in range(2):
-            mx_group(7, n)
-            finish(7, n * 512, (n + 1) * 512)
+        mx_group(4, 0)
+        mx_group(4, 1)
+        finish(4, 0, HDIM)
+        for m in range(5, 8):
+            mx_group(m, 0, pieces=1)
+            mx_group(m, 1, pieces=(2 if m == 7 else 1))

@@ -23,9 +23,7 @@ def tile_stackrnn_pa_kernel(tc, x, hidden, stack_top, Wi, bi, Wh, bh, W0, b0, W1
     nc = tc.nc
     with ExitStack() as ctx:
         keep = ctx.enter_context(tc.tile_pool(name="keep", bufs=1))
-        tp_pool = ctx.enter_context(tc.psum_pool(name="tp", bufs=3))
-        pl_pool = ctx.enter_context(tc.psum_pool(name="pl", bufs=2))
-        mx_pool = ctx.enter_context(tc.psum_pool(name="mx", bufs=3))
+        psum = ctx.enter_context(tc.psum_pool(name="psum", bufs=8))
         ctx.enter_context(tc.manual_schedule())
 
         x_sb = keep.tile([P, NB * IDIM], BF16)
@@ -36,6 +34,7 @@ def tile_stackrnn_pa_kernel(tc, x, hidden, stack_top, Wi, bi, Wh, bh, W0, b0, W1
         w01_sb = keep.tile([P, 2 * 4 * 2 * S], BF16)
         bias_rows = keep.tile([P, HDIM], BF16)
         ones = keep.tile([P, P], BF16)
+        junk = keep.tile([P, 512], BF16)
         ident_f = keep.tile([P, P], F32)
         warm = keep.tile([P, 1], F32)
         stT = keep.tile([P, NB * P * 2], BF16)
@@ -47,8 +46,9 @@ def tile_stackrnn_pa_kernel(tc, x, hidden, stack_top, Wi, bi, Wh, bh, W0, b0, W1
         w_scales = keep.tile([P, PASSES, HDIM], U8, align_bytes=64)
         pre = keep.tile([P, NB, HDIM], F32)
 
-        nc.vector.memset(bias_rows[:], 0.0)
         nc.vector.memset(ones[:], 1.0)
+        nc.vector.memset(junk[:], 0.0)
+        nc.vector.memset(bias_rows[:], 0.0)
         nc.vector.memset(warm[:], 0.0)
         make_identity(nc, ident_f[:])
         for r, b_vec in enumerate((bi, bh, b0, b1)):
@@ -106,7 +106,7 @@ def tile_stackrnn_pa_kernel(tc, x, hidden, stack_top, Wi, bi, Wh, bh, W0, b0, W1
 
         def transposes(job, first, last):
             if first == 0:
-                banks[job] = tp_pool.tile([P, 512], F32, tag="tp", name="tbank")
+                banks[job] = psum.tile([P, 512], F32, tag="bank", name="tbank")
             srcs = sources(*job)
             for i in range(first, last):
                 nc.tensor.transpose(banks[job][:, i * P : (i + 1) * P], srcs[i], ident_f[:])
@@ -142,7 +142,7 @@ def tile_stackrnn_pa_kernel(tc, x, hidden, stack_top, Wi, bi, Wh, bh, W0, b0, W1
         def plain_matmul(group, e):
             m, n = group
             if e == 0:
-                banks[group] = pl_pool.tile([P, 512], F32, tag="pl", name="pbank")
+                banks[group] = psum.tile([P, 512], F32, tag="bank", name="pbank")
             nc.tensor.matmul(banks[group][:], lhsT=stT_e[:, m, :, e], rhs=w01T_e[:, n, :, e], start=(e == 0), stop=(e == 1))
 
         def add_bias(group):
@@ -154,13 +154,18 @@ def tile_stackrnn_pa_kernel(tc, x, hidden, stack_top, Wi, bi, Wh, bh, W0, b0, W1
             transposes(job, 0, len(sources(*job)))
             copy_out(job, on_vector)
 
-        def woven(group, job):
+        def woven(group, job, with_bias=True):
             plain_matmul(group, 0)
             transposes(job, 0, 2)
             plain_matmul(group, 1)
             transposes(job, 2, len(sources(*job)))
             copy_out(job)
-            add_bias(group)
+            if with_bias:
+                add_bias(group)
+
+        def warm_up(count):
+            for i in range(count):
+                nc.tensor.matmul(warm_bank[:], lhsT=ones[:], rhs=junk[:], start=True, stop=True)
 
         def finish(m, first_col, last_col):
             cols = slice(first_col, last_col)
@@ -168,7 +173,7 @@ def tile_stackrnn_pa_kernel(tc, x, hidden, stack_top, Wi, bi, Wh, bh, W0, b0, W1
             nc.sync.dma_start(out=out_v[:, m, cols], in_=pre[:, m, cols])
 
         def mx_group(m, n, pieces=0):
-            bank = mx_pool.tile([P, 512], F32, tag="mx", name="mbank")
+            bank = psum.tile([P, 512], F32, tag="bank", name="mbank")
             rows = slice(m * P, (m + 1) * P)
             cols = slice(n * 512, (n + 1) * 512)
             for c in range(PASSES):
@@ -188,16 +193,21 @@ def tile_stackrnn_pa_kernel(tc, x, hidden, stack_top, Wi, bi, Wh, bh, W0, b0, W1
                 if pieces > 0:
                     finish(m, n * 512 + i * width, n * 512 + (i + 1) * width)
 
+        warm_bank = psum.tile([P, 512], F32, tag="bank", name="wbank")
+        warm_up(6)
+        bank_alone(("v", 0, 0))
+        bank_alone(("s", 0, 0), on_vector=True)
+        warm_up(1)
+        woven((0, 0), ("s", 0, 1), with_bias=False)
+        woven((1, 0), ("s", 0, 2), with_bias=False)
         bias_banks = []
         for n in range(2):
-            bias_banks.append(mx_pool.tile([P, 512], F32, tag="mx", name="bbank"))
+            bias_banks.append(psum.tile([P, 512], F32, tag="bank", name="bbank"))
             nc.tensor.matmul(bias_banks[n][:], lhsT=ones[:], rhs=bias_rows[:, n * 512 : (n + 1) * 512], start=True, stop=True)
         nc.vector.tensor_copy(out=bias_bc[:, 0:512], in_=bias_banks[0][:])
         nc.scalar.copy(out=bias_bc[:, 512:1024], in_=bias_banks[1][:])
-        bank_alone(("v", 0, 0))
-        bank_alone(("s", 0, 0), on_vector=True)
-        woven((0, 0), ("s", 0, 1))
-        woven((1, 0), ("s", 0, 2))
+        add_bias((0, 0))
+        add_bias((1, 0))
         woven((2, 0), ("v", 0, 1))
 
         groups = [(3, 0), (4, 0), (5, 0)] + [(m, 1) for m in range(6)] + [(6, 0), (6, 1), (7, 0), (7, 1)]

@@ -51,9 +51,6 @@ def tile_stackrnn_pa_kernel(tc, x, hidden, stack_top, Wi, bi, Wh, bh, W0, b0, W1
         nc.vector.memset(bias_rows[:], 0.0)
         nc.vector.memset(warm[:], 0.0)
         make_identity(nc, ident_f[:])
-        for r, b_vec in enumerate((bi, bh, b0, b1)):
-            nc.scalar.dma_start(out=bias_rows[r : r + 1, :], in_=b_vec.rearrange("(o n) -> o n", o=1))
-        nc.scalar.activation(out=warm[:], in_=warm[:], func=SIGMOID)
 
         st_v = stack_top.rearrange("(p t) s k -> p (t s k)", t=NB)
         w0_v = W0.rearrange("(n t p) k -> p n t k", n=2, t=4)
@@ -69,6 +66,9 @@ def tile_stackrnn_pa_kernel(tc, x, hidden, stack_top, Wi, bi, Wh, bh, W0, b0, W1
         nc.sync.dma_start(out=w01_t[:, 0, :, 1, :], in_=w1_v[:, 0])
         nc.sync.dma_start(out=st_sb[:, 0:512], in_=st_v[:, 0:512])
         nc.sync.dma_start(out=st_sb[:, 512:2048], in_=st_v[:, 512:2048])
+        for r, b_vec in enumerate((bi, bh, b0, b1)):
+            nc.scalar.dma_start(out=bias_rows[r : r + 1, :], in_=b_vec.rearrange("(o n) -> o n", o=1))
+        nc.scalar.activation(out=warm[:], in_=warm[:], func=SIGMOID)
         nc.sync.dma_start(out=w01_t[:, 1, :, 0, :], in_=w0_v[:, 1])
         nc.sync.dma_start(out=w01_t[:, 1, :, 1, :], in_=w1_v[:, 1])
         for gg in range(2):

@@ -172,13 +172,13 @@ def tile_stackrnn_pa_kernel(tc, x, hidden, stack_top, Wi, bi, Wh, bh, W0, b0, W1
             nc.scalar.activation(out=pre[:, m, cols], in_=pre[:, m, cols], func=SIGMOID)
             nc.sync.dma_start(out=out_v[:, m, cols], in_=pre[:, m, cols])
 
-        def mx_group(m, n, pieces=0):
+        def mx_group(m, first_col, width, finish_now):
             bank = psum.tile([P, 512], F32, tag="bank", name="mbank")
             rows = slice(m * P, (m + 1) * P)
-            cols = slice(n * 512, (n + 1) * 512)
+            cols = slice(first_col, first_col + width)
             for c in range(PASSES):
                 nc.tensor.matmul_mx(
-                    out=bank[:],
+                    out=bank[:, 0:width],
                     lhsT=a_codes[:, c, rows].bitcast(FP8X4),
                     lhsT_scale=a_scales[:, c, rows],
                     rhs=w_codes[:, c, cols].bitcast(FP8X4),
@@ -186,12 +186,9 @@ def tile_stackrnn_pa_kernel(tc, x, hidden, stack_top, Wi, bi, Wh, bh, W0, b0, W1
                     start=(c == 0),
                     stop=(c == PASSES - 1),
                 )
-            width = 512 // max(pieces, 1)
-            for i in range(max(pieces, 1)):
-                part = slice(n * 512 + i * width, n * 512 + (i + 1) * width)
-                nc.vector.tensor_tensor(out=pre[:, m, part], in0=bank[:, i * width : (i + 1) * width], in1=pre[:, m, part], op=ADD)
-                if pieces > 0:
-                    finish(m, n * 512 + i * width, n * 512 + (i + 1) * width)
+            nc.vector.tensor_tensor(out=pre[:, m, cols], in0=bank[:, 0:width], in1=pre[:, m, cols], op=ADD)
+            if finish_now:
+                finish(m, first_col, first_col + width)
 
         warm_bank = psum.tile([P, 512], F32, tag="bank", name="wbank")
         warm_up(6)
@@ -230,8 +227,8 @@ def tile_stackrnn_pa_kernel(tc, x, hidden, stack_top, Wi, bi, Wh, bh, W0, b0, W1
             gi += 1
             quantise(job_b)
         for m in range(4):
-            mx_group(m, 0)
-            mx_group(m, 1)
+            mx_group(m, 0, 512, False)
+            mx_group(m, 512, 512, False)
             if m < 3:
                 finish(m, 0, HDIM)
         for i in range(EARLY, len(chunks)):
@@ -242,9 +239,13 @@ def tile_stackrnn_pa_kernel(tc, x, hidden, stack_top, Wi, bi, Wh, bh, W0, b0, W1
             quantise(job_a)
             quantise(job_b)
         finish(3, 0, HDIM)
-        mx_group(4, 0)
-        mx_group(4, 1)
+        mx_group(4, 0, 512, False)
+        mx_group(4, 512, 512, False)
         finish(4, 0, HDIM)
-        for m in range(5, 8):
-            mx_group(m, 0, pieces=1)
-            mx_group(m, 1, pieces=(2 if m == 7 else 1))
+        for m in (5, 6):
+            mx_group(m, 0, 512, True)
+            mx_group(m, 512, 512, True)
+        mx_group(7, 0, 512, True)
+        mx_group(7, 512, 256, True)
+        mx_group(7, 768, 128, True)
+        mx_group(7, 896, 128, True)

@@ -33,7 +33,7 @@ def tile_stackrnn_pa_kernel(tc, x, hidden, stack_top, Wi, bi, Wh, bh, W0, b0, W1
         wh_sb = keep.tile([P, 8 * HDIM], BF16)
         w01_sb = keep.tile([P, 2 * 4 * 2 * S], BF16)
         bias_rows = keep.tile([P, HDIM], BF16)
-        ones = keep.tile([P, P], BF16)
+        eighth = keep.tile([P, P], BF16)
         junk = keep.tile([P, 512], BF16)
         ident_f = keep.tile([P, P], F32)
         warm = keep.tile([P, 1], F32)
@@ -46,11 +46,15 @@ def tile_stackrnn_pa_kernel(tc, x, hidden, stack_top, Wi, bi, Wh, bh, W0, b0, W1
         w_scales = keep.tile([P, PASSES, HDIM], U8, align_bytes=64)
         pre = keep.tile([P, NB, HDIM], F32)
 
-        nc.vector.memset(ones[:], 1.0)
+        for r, b_vec in enumerate((bi, bh, b0, b1)):
+            nc.scalar.dma_start(out=bias_rows[8 * r : 8 * r + 8, :], in_=b_vec.partition_broadcast(8))
+        nc.vector.memset(eighth[:], 0.125)
         nc.vector.memset(junk[:], 0.0)
-        nc.vector.memset(bias_rows[:], 0.0)
         nc.vector.memset(warm[:], 0.0)
+        nc.vector.memset(bias_rows[32:64, :], 0.0)
+        nc.vector.memset(bias_rows[64:128, :], 0.0)
         make_identity(nc, ident_f[:])
+        nc.scalar.activation(out=warm[:], in_=warm[:], func=SIGMOID)
 
         st_v = stack_top.rearrange("(p t) s k -> p (t s k)", t=NB)
         w0_v = W0.rearrange("(n t p) k -> p n t k", n=2, t=4)
@@ -66,9 +70,6 @@ def tile_stackrnn_pa_kernel(tc, x, hidden, stack_top, Wi, bi, Wh, bh, W0, b0, W1
         nc.sync.dma_start(out=w01_t[:, 0, :, 1, :], in_=w1_v[:, 0])
         nc.sync.dma_start(out=st_sb[:, 0:512], in_=st_v[:, 0:512])
         nc.sync.dma_start(out=st_sb[:, 512:2048], in_=st_v[:, 512:2048])
-        for r, b_vec in enumerate((bi, bh, b0, b1)):
-            nc.scalar.dma_start(out=bias_rows[r : r + 1, :], in_=b_vec.rearrange("(o n) -> o n", o=1))
-        nc.scalar.activation(out=warm[:], in_=warm[:], func=SIGMOID)
         nc.sync.dma_start(out=w01_t[:, 1, :, 0, :], in_=w0_v[:, 1])
         nc.sync.dma_start(out=w01_t[:, 1, :, 1, :], in_=w1_v[:, 1])
         for gg in range(2):
@@ -165,20 +166,20 @@ def tile_stackrnn_pa_kernel(tc, x, hidden, stack_top, Wi, bi, Wh, bh, W0, b0, W1
 
         def warm_up(count):
             for i in range(count):
-                nc.tensor.matmul(warm_bank[:], lhsT=ones[:], rhs=junk[:], start=True, stop=True)
+                nc.tensor.matmul(warm_bank[:], lhsT=eighth[:], rhs=junk[:], start=True, stop=True)
 
         def finish(m, first_col, last_col):
             cols = slice(first_col, last_col)
             nc.scalar.activation(out=pre[:, m, cols], in_=pre[:, m, cols], func=SIGMOID)
             nc.sync.dma_start(out=out_v[:, m, cols], in_=pre[:, m, cols])
 
-        def mx_group(m, first_col, width, finish_now):
+        def mx_group(m, n, pieces=0):
             bank = psum.tile([P, 512], F32, tag="bank", name="mbank")
             rows = slice(m * P, (m + 1) * P)
-            cols = slice(first_col, first_col + width)
+            cols = slice(n * 512, (n + 1) * 512)
             for c in range(PASSES):
                 nc.tensor.matmul_mx(
-                    out=bank[:, 0:width],
+                    out=bank[:],
                     lhsT=a_codes[:, c, rows].bitcast(FP8X4),
                     lhsT_scale=a_scales[:, c, rows],
                     rhs=w_codes[:, c, cols].bitcast(FP8X4),
@@ -186,25 +187,25 @@ def tile_stackrnn_pa_kernel(tc, x, hidden, stack_top, Wi, bi, Wh, bh, W0, b0, W1
                     start=(c == 0),
                     stop=(c == PASSES - 1),
                 )
-            nc.vector.tensor_tensor(out=pre[:, m, cols], in0=bank[:, 0:width], in1=pre[:, m, cols], op=ADD)
-            if finish_now:
-                finish(m, first_col, first_col + width)
+            width = 512 // max(pieces, 1)
+            for i in range(max(pieces, 1)):
+                part = slice(n * 512 + i * width, n * 512 + (i + 1) * width)
+                nc.vector.tensor_tensor(out=pre[:, m, part], in0=bank[:, i * width : (i + 1) * width], in1=pre[:, m, part], op=ADD)
+                if pieces > 0:
+                    finish(m, n * 512 + i * width, n * 512 + (i + 1) * width)
 
         warm_bank = psum.tile([P, 512], F32, tag="bank", name="wbank")
         warm_up(6)
         bank_alone(("v", 0, 0))
         bank_alone(("s", 0, 0), on_vector=True)
-        warm_up(1)
-        woven((0, 0), ("s", 0, 1), with_bias=False)
-        woven((1, 0), ("s", 0, 2), with_bias=False)
         bias_banks = []
         for n in range(2):
             bias_banks.append(psum.tile([P, 512], F32, tag="bank", name="bbank"))
-            nc.tensor.matmul(bias_banks[n][:], lhsT=ones[:], rhs=bias_rows[:, n * 512 : (n + 1) * 512], start=True, stop=True)
+            nc.tensor.matmul(bias_banks[n][:], lhsT=eighth[:], rhs=bias_rows[:, n * 512 : (n + 1) * 512], start=True, stop=True)
         nc.vector.tensor_copy(out=bias_bc[:, 0:512], in_=bias_banks[0][:])
         nc.scalar.copy(out=bias_bc[:, 512:1024], in_=bias_banks[1][:])
-        add_bias((0, 0))
-        add_bias((1, 0))
+        woven((0, 0), ("s", 0, 1))
+        woven((1, 0), ("s", 0, 2))
         woven((2, 0), ("v", 0, 1))
 
         groups = [(3, 0), (4, 0), (5, 0)] + [(m, 1) for m in range(6)] + [(6, 0), (6, 1), (7, 0), (7, 1)]
@@ -227,8 +228,8 @@ def tile_stackrnn_pa_kernel(tc, x, hidden, stack_top, Wi, bi, Wh, bh, W0, b0, W1
             gi += 1
             quantise(job_b)
         for m in range(4):
-            mx_group(m, 0, 512, False)
-            mx_group(m, 512, 512, False)
+            mx_group(m, 0)
+            mx_group(m, 1)
             if m < 3:
                 finish(m, 0, HDIM)
         for i in range(EARLY, len(chunks)):
@@ -239,13 +240,9 @@ def tile_stackrnn_pa_kernel(tc, x, hidden, stack_top, Wi, bi, Wh, bh, W0, b0, W1
             quantise(job_a)
             quantise(job_b)
         finish(3, 0, HDIM)
-        mx_group(4, 0, 512, False)
-        mx_group(4, 512, 512, False)
+        mx_group(4, 0)
+        mx_group(4, 1)
         finish(4, 0, HDIM)
-        for m in (5, 6):
-            mx_group(m, 0, 512, True)
-            mx_group(m, 512, 512, True)
-        mx_group(7, 0, 512, True)
-        mx_group(7, 512, 256, True)
-        mx_group(7, 768, 128, True)
-        mx_group(7, 896, 128, True)
+        for m in range(5, 8):
+            mx_group(m, 0, pieces=1)
+            mx_group(m, 1, pieces=(2 if m == 7 else 1))

from contextlib import ExitStack

import concourse.mybir as mybir
from concourse.masks import make_identity

F32 = mybir.dt.float32
BF16 = mybir.dt.bfloat16
U32 = mybir.dt.uint32
U8 = mybir.dt.uint8
FP8X4 = mybir.dt.float8_e4m3fn_x4
ADD = mybir.AluOpType.add
SIGMOID = mybir.ActivationFunctionType.Sigmoid

P = 128
B, IDIM, HDIM, S = 1024, 512, 1024, 128
NB = B // P
PASSES = 3
ST_SLOTS = ((0, 1), (2, 3, 4, 5), (6, 7))
FLOPS = 2 * B * HDIM * (IDIM + HDIM + 2 * S)


def tile_stackrnn_pa_kernel(tc, x, hidden, stack_top, Wi, bi, Wh, bh, W0, b0, W1, b1, out):
    nc = tc.nc
    with ExitStack() as ctx:
        keep = ctx.enter_context(tc.tile_pool(name="keep", bufs=1))
        psum = ctx.enter_context(tc.psum_pool(name="psum", bufs=8))
        ctx.enter_context(tc.manual_schedule())

        x_sb = keep.tile([P, NB * IDIM], BF16)
        h_sb = keep.tile([P, NB * HDIM], BF16)
        st_sb = keep.tile([P, NB * 2 * S], BF16)
        wi_sb = keep.tile([P, 8 * IDIM], BF16)
        wh_sb = keep.tile([P, 8 * HDIM], BF16)
        w01_sb = keep.tile([P, 2 * 4 * 2 * S], BF16)
        bias_rows = keep.tile([P, HDIM], BF16)
        eighth = keep.tile([P, P], BF16)
        junk = keep.tile([P, 512], BF16)
        ident_f = keep.tile([P, P], F32)
        warm = keep.tile([P, 1], F32)
        stT = keep.tile([P, NB * P * 2], BF16)
        w01T = keep.tile([P, HDIM * 2], BF16)
        bias_bc = keep.tile([P, HDIM], F32)
        a_codes = keep.tile([P, PASSES, B], U32, align_bytes=64)
        a_scales = keep.tile([P, PASSES, B], U8, align_bytes=64)
        w_codes = keep.tile([P, PASSES, HDIM], U32, align_bytes=64)
        w_scales = keep.tile([P, PASSES, HDIM], U8, align_bytes=64)
        pre = keep.tile([P, NB, HDIM], F32)

        for r, b_vec in enumerate((bi, bh, b0, b1)):
            nc.scalar.dma_start(out=bias_rows[8 * r : 8 * r + 8, :], in_=b_vec.partition_broadcast(8))
        nc.vector.memset(eighth[:], 0.125)
        nc.vector.memset(junk[:], 0.0)
        nc.vector.memset(warm[:], 0.0)
        nc.vector.memset(bias_rows[32:64, :], 0.0)
        nc.vector.memset(bias_rows[64:128, :], 0.0)
        make_identity(nc, ident_f[:])
        nc.scalar.activation(out=warm[:], in_=warm[:], func=SIGMOID)

        st_v = stack_top.rearrange("(p t) s k -> p (t s k)", t=NB)
        w0_v = W0.rearrange("(n t p) k -> p n t k", n=2, t=4)
        w1_v = W1.rearrange("(n t p) k -> p n t k", n=2, t=4)
        w01_t = w01_sb[:].rearrange("p (n t s k) -> p n t s k", n=2, t=4, s=2)
        x_v = x.rearrange("(p t) k -> p (t k)", t=NB)
        h_v = hidden.rearrange("(p t) k -> p (t k)", t=NB)
        wi_v = Wi.rearrange("(g p t) k -> p g (t k)", g=4, t=2)
        wh_v = Wh.rearrange("(g p t) k -> p g (t k)", g=4, t=2)
        wi_t = wi_sb[:].rearrange("p (g c) -> p g c", g=4)

        nc.sync.dma_start(out=w01_t[:, 0, :, 0, :], in_=w0_v[:, 0])
        nc.sync.dma_start(out=w01_t[:, 0, :, 1, :], in_=w1_v[:, 0])
        nc.sync.dma_start(out=st_sb[:, 0:512], in_=st_v[:, 0:512])
        nc.sync.dma_start(out=st_sb[:, 512:2048], in_=st_v[:, 512:2048])
        nc.sync.dma_start(out=w01_t[:, 1, :, 0, :], in_=w0_v[:, 1])
        nc.sync.dma_start(out=w01_t[:, 1, :, 1, :], in_=w1_v[:, 1])
        for gg in range(2):
            nc.sync.dma_start(out=wi_t[:, 2 * gg : 2 * gg + 2, :], in_=wi_v[:, 2 * gg : 2 * gg + 2, :])
            for g in (2 * gg, 2 * gg + 1):
                nc.sync.dma_start(out=wh_sb[:, g * 2048 : (g + 1) * 2048], in_=wh_v[:, g, :])
        for hh in range(2):
            nc.sync.dma_start(out=x_sb[:, hh * 2048 : (hh + 1) * 2048], in_=x_v[:, hh * 2048 : (hh + 1) * 2048])
            for pr in (2 * hh, 2 * hh + 1):
                nc.sync.dma_start(out=h_sb[:, pr * 2048 : (pr + 1) * 2048], in_=h_v[:, pr * 2048 : (pr + 1) * 2048])

        words = {"s": st_sb[:].bitcast(F32), "v": w01_sb[:].bitcast(F32)}
        mx_words = {("a", 0): x_sb[:].bitcast(F32), ("a", 1): h_sb[:].bitcast(F32), ("w", 0): wi_sb[:].bitcast(F32), ("w", 1): wh_sb[:].bitcast(F32)}
        stT_w = stT[:].bitcast(F32)
        w01T_w = w01T[:].bitcast(F32)
        stT_e = stT[:].rearrange("p (t j e) -> p t j e", t=NB, e=2)
        w01T_e = w01T[:].rearrange("p (n h e) -> p n h e", n=2, e=2)
        out_v = out.rearrange("(p t) h -> p t h", t=NB)
        grouped = {}
        banks = {}

        def sources(kind, c, q):
            if kind == "s":
                return [words[kind][:, t * P : (t + 1) * P] for t in ST_SLOTS[q]]
            if kind == "v":
                return [words[kind][:, (4 * q + i) * P : (4 * q + i + 1) * P] for i in range(4)]
            src = mx_words[(kind, min(c, 1))]
            row_words = IDIM // 2 if c == 0 else HDIM // 2
            off = 0 if c == 0 else (c - 1) * 256
            return [
                src[:, (2 * q + r) * row_words + off + u * P : (2 * q + r) * row_words + off + (u + 1) * P]
                for r in range(2)
                for u in range(2)
            ]

        def transposes(job, first, last):
            if first == 0:
                banks[job] = psum.tile([P, 512], F32, tag="bank", name="tbank")
            srcs = sources(*job)
            for i in range(first, last):
                nc.tensor.transpose(banks[job][:, i * P : (i + 1) * P], srcs[i], ident_f[:])

        def copy_out(job, on_vector=False):
            kind, c, q = job
            bank = banks[job]
            if kind == "s":
                slots = ST_SLOTS[q]
                dst, src = stT_w[:, slots[0] * P : (slots[-1] + 1) * P], bank[:, 0 : len(slots) * P]
            elif kind == "v":
                dst, src = w01T_w[:, q * 512 : (q + 1) * 512], bank[:]
            else:
                grouped[job] = keep.tile([P, 1024], BF16, align_bytes=64, name="grp_%s%d%d" % job)
                gw = grouped[job][:].bitcast(F32)
                if kind == "a":
                    dst = gw.rearrange("p (r j u) -> p r j u", r=2, u=2)
                    src = bank[:].rearrange("p (r u j) -> p r j u", r=2, u=2)
                else:
                    dst = gw.rearrange("p (j r u) -> p j r u", r=2, u=2)
                    src = bank[:].rearrange("p (r u j) -> p j r u", r=2, u=2)
            if on_vector:
                nc.vector.tensor_copy(out=dst, in_=src)
            else:
                nc.scalar.copy(out=dst, in_=src)

        def quantise(job):
            kind, c, q = job
            codes, scales = (a_codes, a_scales) if kind == "a" else (w_codes, w_scales)
            cols = slice(q * 256, (q + 1) * 256)
            nc.vector.quantize_mx(out=codes[:, c, cols].bitcast(FP8X4), scales=scales[:, c, cols], in_=grouped[job][:])

        def plain_matmul(group, e):
            m, n = group
            if e == 0:
                banks[group] = psum.tile([P, 512], F32, tag="bank", name="pbank")
            nc.tensor.matmul(banks[group][:], lhsT=stT_e[:, m, :, e], rhs=w01T_e[:, n, :, e], start=(e == 0), stop=(e == 1))

        def add_bias(group):
            m, n = group
            cols = slice(n * 512, (n + 1) * 512)
            nc.vector.tensor_tensor(out=pre[:, m, cols], in0=banks[group][:], in1=bias_bc[:, cols], op=ADD)

        def bank_alone(job, on_vector=False):
            transposes(job, 0, len(sources(*job)))
            copy_out(job, on_vector)

        def woven(group, job, with_bias=True):
            plain_matmul(group, 0)
            transposes(job, 0, 2)
            plain_matmul(group, 1)
            transposes(job, 2, len(sources(*job)))
            copy_out(job)
            if with_bias:
                add_bias(group)

        def warm_up(count):
            for i in range(count):
                nc.tensor.matmul(warm_bank[:], lhsT=eighth[:], rhs=junk[:], start=True, stop=True)

        def finish(m, first_col, last_col):
            cols = slice(first_col, last_col)
            nc.scalar.activation(out=pre[:, m, cols], in_=pre[:, m, cols], func=SIGMOID)
            nc.sync.dma_start(out=out_v[:, m, cols], in_=pre[:, m, cols])

        def mx_group(m, n, pieces=0):
            bank = psum.tile([P, 512], F32, tag="bank", name="mbank")
            rows = slice(m * P, (m + 1) * P)
            cols = slice(n * 512, (n + 1) * 512)
            for c in range(PASSES):
                nc.tensor.matmul_mx(
                    out=bank[:],
                    lhsT=a_codes[:, c, rows].bitcast(FP8X4),
                    lhsT_scale=a_scales[:, c, rows],
                    rhs=w_codes[:, c, cols].bitcast(FP8X4),
                    rhs_scale=w_scales[:, c, cols],
                    start=(c == 0),
                    stop=(c == PASSES - 1),
                )
            width = 512 // max(pieces, 1)
            for i in range(max(pieces, 1)):
                part = slice(n * 512 + i * width, n * 512 + (i + 1) * width)
                nc.vector.tensor_tensor(out=pre[:, m, part], in0=bank[:, i * width : (i + 1) * width], in1=pre[:, m, part], op=ADD)
                if pieces > 0:
                    finish(m, n * 512 + i * width, n * 512 + (i + 1) * width)

        warm_bank = psum.tile([P, 512], F32, tag="bank", name="wbank")
        warm_up(6)
        bank_alone(("v", 0, 0))
        bank_alone(("s", 0, 0), on_vector=True)
        bias_banks = []
        for n in range(2):
            bias_banks.append(psum.tile([P, 512], F32, tag="bank", name="bbank"))
            nc.tensor.matmul(bias_banks[n][:], lhsT=eighth[:], rhs=bias_rows[:, n * 512 : (n + 1) * 512], start=True, stop=True)
        nc.vector.tensor_copy(out=bias_bc[:, 0:512], in_=bias_banks[0][:])
        nc.scalar.copy(out=bias_bc[:, 512:1024], in_=bias_banks[1][:])
        woven((0, 0), ("s", 0, 1))
        woven((1, 0), ("s", 0, 2))
        woven((2, 0), ("v", 0, 1))

        groups = [(3, 0), (4, 0), (5, 0)] + [(m, 1) for m in range(6)] + [(6, 0), (6, 1), (7, 0), (7, 1)]
        chunks = []
        for kind in ("w", "a"):
            for hh in range(2):
                chunks.append([(kind, 0, 2 * hh), (kind, 0, 2 * hh + 1)])
                for q in (2 * hh, 2 * hh + 1):
                    chunks.append([(kind, 1, q), (kind, 2, q)])
        EARLY = 10
        plain_matmul(groups[0], 0)
        plain_matmul(groups[0], 1)
        add_bias(groups[0])
        gi = 1
        for i in range(EARLY):
            job_a, job_b = chunks[i]
            bank_alone(job_a)
            quantise(job_a)
            woven(groups[gi], job_b)
            gi += 1
            quantise(job_b)
        for m in range(4):
            mx_group(m, 0)
            mx_group(m, 1)
            if m < 3:
                finish(m, 0, HDIM)
        for i in range(EARLY, len(chunks)):
            job_a, job_b = chunks[i]
            bank_alone(job_a)
            woven(groups[gi], job_b)
            gi += 1
            quantise(job_a)
            quantise(job_b)
        finish(3, 0, HDIM)
        mx_group(4, 0)
        mx_group(4, 1)
        finish(4, 0, HDIM)
        for m in range(5, 8):
            mx_group(m, 0, pieces=1)
            mx_group(m, 1, pieces=(2 if m == 7 else 1))
